import numpy as np
import ml_dtypes


def mxq(x, axis, fmt="e4m3"):
    dtype, down = {"e4m3": (ml_dtypes.float8_e4m3fn, 7), "e5m2": (ml_dtypes.float8_e5m2, 14)}[fmt]
    v = np.moveaxis(np.asarray(x, np.float32).astype(ml_dtypes.bfloat16).astype(np.float64), axis, -1)
    blocks = v.reshape(v.shape[:-1] + (-1, 32))
    amax = np.abs(blocks).max(-1, keepdims=True)
    byte = np.maximum(np.where(amax > 0, np.frexp(amax)[1] - 1 + 127, 0) - down, 1)
    scale = np.exp2(byte - 127.0)
    codes = (blocks / scale).astype(np.float32).astype(dtype).astype(np.float64)
    return np.moveaxis((codes * scale).reshape(v.shape), -1, axis)


WIDE = False


def mx_kscale(k):
    if not WIDE:
        return np.ones(k)
    levels = np.array([10, -10, 5, -5, 0])
    if k % 512:
        return np.exp2(np.random.permutation(np.resize(levels, k // 32))).repeat(32)
    a = np.empty((k // 512, 16))
    for p in range(k // 512):
        a[p, :8] = np.random.permutation(np.resize(levels, 8))
        for g in range(8):
            far = levels[np.abs(levels - a[p, g]) >= 10]
            a[p, g + 8] = far[np.random.randint(len(far))]
    return np.exp2(a.ravel()).repeat(32)


BF16 = ml_dtypes.bfloat16


def bf(x):
    return np.asarray(x, np.float32).astype(BF16)


def f64(x):
    return np.asarray(x).astype(np.float64)


B, S, DIM, QL, KVL, H, DN, DR, DV, P0 = 2, 256, 2048, 1536, 512, 16, 128, 128, 128, 37
EPS = 1e-6
HALF = DR // 2


def rms_norm(v, w):
    return v / np.sqrt(np.mean(v * v, axis=-1, keepdims=True) + EPS) * w


def rope(v, start):
    theta = 10000.0 ** (-np.arange(HALF) / HALF)
    pos = np.arange(v.shape[-2]) + start
    ang = pos[:, None] * theta[None, :]
    ang2 = np.concatenate([ang, ang], axis=-1)
    v1, v2 = v[..., :HALF], v[..., HALF:]
    rot = np.concatenate([-v2, v1], axis=-1)
    return v * np.cos(ang2) + rot * np.sin(ang2)


def draw0():
    s, t = mx_kscale(DIM), mx_kscale(QL)
    return {"x": bf(np.random.standard_normal((B, S, DIM)) * s),
            "wq_a": bf(np.random.standard_normal((DIM, QL)) / np.sqrt(DIM) / s[:, None]),
            "q_norm_w": bf((1.0 + 0.1 * np.random.standard_normal(QL)) * t),
            "wq_b": bf(np.random.standard_normal((QL, H * (DN + DR))) / np.sqrt(QL) / t[:, None])}


def core(x, wq_a, q_norm_w, wq_b):
    c = mxq(f64(x), 2, "e4m3") @ mxq(f64(wq_a), 0, "e4m3")
    cn = rms_norm(c, f64(q_norm_w))
    q = (mxq(cn, 2, "e4m3") @ mxq(f64(wq_b), 0, "e4m3")).reshape(B, S, H, DN + DR)
    q_nope, q_rope = q[..., :DN], q[..., DN:]
    q_rope = rope(q_rope.reshape(B, H, S, DR), P0).reshape(B, S, H, DR)
    return np.concatenate([q_nope, q_rope], axis=-1)


def e4m3fn_bytes(y):
    return np.clip(np.asarray(y, np.float64), -448.0, 448.0).astype(np.float32).astype(ml_dtypes.float8_e4m3fn).view(np.uint8)


def e4m3fn_values(b):
    return np.asarray(b, np.uint8).view(ml_dtypes.float8_e4m3fn).astype(np.float64)


def setup_inputs():
    d = draw0()
    x0 = np.asarray(d['wq_b']).astype(np.float64)
    s = (np.max(np.abs(x0), axis=(1,), keepdims=True) / 448.0).astype(np.float32)
    out = {}
    for k, v in d.items():
        if k == 'wq_b':
            out['wq_b_bytes'] = e4m3fn_bytes(x0 / s.astype(np.float64))
            out['wq_b_scale'] = s
        else:
            out[k] = v
    return out


def reference(x, wq_a, q_norm_w, wq_b_bytes, wq_b_scale):
    return core(x, wq_a, q_norm_w, e4m3fn_values(wq_b_bytes) * wq_b_scale.astype(np.float64))

@@ -1,0 +1,422 @@
+import math
+from contextlib import ExitStack
+
+import concourse.mybir as mybir
+from concourse.masks import make_identity
+
+F32 = mybir.dt.float32
+BF16 = mybir.dt.bfloat16
+I32 = mybir.dt.int32
+U32 = mybir.dt.uint32
+U8 = mybir.dt.uint8
+FP8 = mybir.dt.float8_e4m3fn
+FP8X4 = mybir.dt.float8_e4m3fn_x4
+ALU = mybir.AluOpType
+ACT = mybir.ActivationFunctionType
+
+P = 128
+TOK, DIM, QL, OUT = 512, 2048, 1536, 4096
+HEADS, HD, DR = 16, 256, 128
+HALF = DR // 2
+POS0 = 37
+EPS = 1e-6
+FLOPS = 2 * TOK * DIM * QL + 2 * TOK * QL * OUT
+
+MT = TOK // P
+G1 = DIM // 512
+G2 = QL // 512
+NQ = 4
+QW = OUT // NQ
+
+UNITS = [(q, g) for q in range(NQ) for g in range(G2)]
+PE_UNITS = {(1, 1), (1, 2), (2, 1), (2, 2), (3, 1), (3, 2)}
+V_WIDEN = [4, 2, 0, 1, 3, 3, 0, 2, 2, 0, 1, 2]
+S_CHUNKS = {(0, 1), (1, 2), (2, 0), (3, 1), (3, 2)}
+
+X_AT = [0, 1, 2, 3]
+ADV0 = 4
+ADV1 = [0, 0, 0, 0, 0, 0, 0, 0, 0, 1, 0, 0]
+ADVN = [1, 6, 2, 2, 4, 4, 2]
+ADVB = [2, 3, 1, 3, 2, 3, 0, 1, 2, 2, 2, 0, 2, 1, 4, 4]
+GP_ADDS = (12, 13, 14, 15)
+EARLY_UNITS = 5
+QUANT_AT = 2
+TAB_AT = 9
+
+
+def tile_mla_pa_kernel(tc, x, wq_a, q_norm_w, wq_b_bytes, wq_b_scale, out):
+    nc = tc.nc
+    x_rows = x.rearrange("b s d -> (b s) d")
+    out_rows = out.rearrange("b s h c -> (b s) (h c)")
+
+    with ExitStack() as ctx:
+        const = ctx.enter_context(tc.tile_pool(name="const", bufs=1))
+        wb = ctx.enter_context(tc.tile_pool(name="wb", bufs=1))
+        psum = ctx.enter_context(tc.psum_pool(name="psum", bufs=1))
+        ctx.enter_context(tc.manual_schedule())
+
+        sc = const.tile([P, G2, 4], F32, name="sc")
+        byte_tiles, plane_tiles, group_tiles, wb_codes = {}, {}, {}, {}
+        loaded, late = [], []
+
+        def load_bytes():
+            if len(loaded) == len(UNITS):
+                return
+            q, g = UNITS[len(loaded)]
+            b = wb.tile([P, 4, QW], U8, name="wbytes", bufs=5)
+            rows = wq_b_bytes[g * 512:(g + 1) * 512, q * QW:(q + 1) * QW]
+            nc.sync.dma_start(out=b[:], in_=rows.rearrange("(p t) n -> p t n", t=4))
+            byte_tiles[(q, g)] = b
+            loaded.append((q, g))
+
+        def widen(k, t):
+            q, g = UNITS[k]
+            if t == 0:
+                plane_tiles[k] = wb.tile([P, 4, QW], BF16, name="planes", bufs=3, align_bytes=64)
+            planes = plane_tiles[k]
+            src = byte_tiles[(q, g)][:, t, :].bitcast(FP8)
+            if t < V_WIDEN[k]:
+                nc.vector.tensor_scalar(out=planes[:, t, :], in0=src, scalar1=sc[:, g, t:t + 1], scalar2=None, op0=ALU.mult)
+            else:
+                nc.scalar.activation(out=planes[:, t, :], in_=src, func=ACT.Copy, scale=sc[:, g, t:t + 1])
+
+        def interleave(eng, dst, src):
+            d = dst.rearrange("p (c i t) -> p c t i", i=4, t=4)
+            s = src.rearrange("p t (c i) -> p c t i", i=4)
+            if eng == "v":
+                nc.vector.tensor_copy(out=d, in_=s)
+            else:
+                nc.scalar.copy(out=d, in_=s)
+
+        def part(k, j):
+            if j == 0:
+                group_tiles[k] = wb.tile([P, 4 * QW], BF16, name="grp", bufs=3, align_bytes=64)
+            planes, grp = plane_tiles[k], group_tiles[k]
+            if UNITS[k] in PE_UNITS:
+                bank = psum.tile([P, 1024], BF16, name="tp", bufs=2)
+                for i in range(2):
+                    c0 = 256 * j + 128 * i
+                    nc.tensor.matmul(bank[:, 512 * i:512 * (i + 1)], lhsT=ident_b[:],
+                                     rhs=planes[:, :, c0:c0 + 128].rearrange("p t c -> p c t"), start=True, stop=True)
+                nc.scalar.copy(out=grp[:, 1024 * j:1024 * (j + 1)], in_=bank[:])
+            elif j % 2 == 1:
+                interleave("v", grp[:, 1024 * (j - 1):1024 * (j + 1)], planes[:, :, 256 * (j - 1):256 * (j + 1)])
+
+        def quantise_unit(k):
+            pool = wb if k < EARLY_UNITS else late[0]
+            codes = pool.tile([P, QW], U32, name="wbc%d" % k, align_bytes=64)
+            scales = pool.tile([P, QW], U8, name="wbs%d" % k, align_bytes=64)
+            nc.vector.quantize_mx(out=codes[:].bitcast(FP8X4), scales=scales[:], in_=group_tiles[k][:])
+            wb_codes[UNITS[k]] = (codes, scales)
+
+        STEPS = 4 + 4 * len(UNITS) + 1
+        done = []
+
+        def background(s):
+            if s < 4:
+                widen(0, s)
+                return
+            k, j = divmod(s - 4, 4)
+            if k == len(UNITS):
+                quantise_unit(k - 1)
+                return
+            if k + 1 < len(UNITS):
+                widen(k + 1, j)
+            part(k, j)
+            if j == QUANT_AT and k > 0:
+                quantise_unit(k - 1)
+                load_bytes()
+
+        def advance(n):
+            for _ in range(min(n, STEPS - len(done))):
+                background(len(done))
+                done.append(0)
+
+        def upto_unit(k):
+            while UNITS[k] not in wb_codes:
+                advance(1)
+
+        with tc.tile_pool(name="p1", bufs=1) as p1:
+            nc.sync.dma_start(out=sc[:], in_=wq_b_scale.rearrange("(g p t) o -> p g (t o)", p=P, t=4))
+            x_raw, wa_raw = [], []
+
+            def load_x():
+                m = len(x_raw)
+                r = p1.tile([P, DIM], BF16, name="xraw", bufs=4)
+                nc.sync.dma_start(out=r[:], in_=x_rows[m * P:(m + 1) * P, :])
+                x_raw.append(r)
+
+            def load_wa():
+                g = len(wa_raw)
+                r = p1.tile([P, 4, QL], BF16, name="waraw", bufs=2)
+                nc.sync.dma_start(out=r[:], in_=wq_a[g * 512:(g + 1) * 512, :].rearrange("(p t) n -> p t n", t=4))
+                wa_raw.append(r)
+
+            load_bytes()
+            load_wa()
+            load_x()
+            load_x()
+            load_x()
+            load_x()
+            load_wa()
+            wrow = p1.tile([P, QL], BF16, name="wrow", align_bytes=64)
+            nc.gpsimd.memset(wrow[:], 0.0)
+            nc.sync.dma_start(out=wrow[0:1, :], in_=q_norm_w.rearrange("(o n) -> o n", o=1))
+
+            ident_f = const.tile([P, P], F32, name="ident_f")
+            make_identity(nc, ident_f[:])
+            ones_b = const.tile([P, P], BF16, name="ones_b")
+            nc.gpsimd.memset(ones_b[:], 1.0)
+            nhalf = const.tile([P, 1], F32, name="nhalf")
+            nc.gpsimd.memset(nhalf[:], -0.5)
+
+            freq = const.tile([P, HALF], F32, name="freq")
+            posi = const.tile([P, HEADS], I32, name="posi")
+            posm = const.tile([P, HEADS], I32, name="posm")
+            post = const.tile([P, HEADS], F32, name="post")
+            nc.gpsimd.iota(posi[:], pattern=[[1, HEADS]], base=0, channel_multiplier=16)
+            nc.vector.memset(freq[:, 0:1], 1.0)
+            n = 1
+            while n < HALF:
+                nc.vector.tensor_scalar(out=freq[:, n:2 * n], in0=freq[:, 0:n], scalar1=10000.0 ** (-n / HALF), scalar2=None, op0=ALU.mult)
+                n *= 2
+            nc.vector.tensor_scalar(out=posm[:], in0=posi[:], scalar1=255, scalar2=None, op0=ALU.bitwise_and)
+            nc.vector.tensor_scalar(out=post[:], in0=posm[:], scalar1=float(POS0), scalar2=1.0 / (2.0 * math.pi), op0=ALU.add, op1=ALU.mult)
+            tmp = wb.tile([P, 2, HEADS, HALF], F32, name="planes", bufs=3, align_bytes=64)
+            whole = p1.tile([P, HEADS, HALF], I32, name="wagrp", bufs=4, align_bytes=64)
+            nc.gpsimd.tensor_tensor(
+                out=tmp[:, 0],
+                in0=post[:].unsqueeze(2).to_broadcast([P, HEADS, HALF]),
+                in1=freq[:].unsqueeze(1).to_broadcast([P, HEADS, HALF]),
+                op=ALU.mult,
+            )
+            nc.vector.tensor_copy(out=whole[:], in_=tmp[:, 0])
+            nc.vector.tensor_tensor(out=tmp[:, 1], in0=tmp[:, 0], in1=whole[:], op=ALU.subtract)
+            ident_b = const.tile([P, P], BF16, name="ident_b")
+            nc.vector.tensor_copy(out=ident_b[:], in_=ident_f[:])
+            tab = const.tile([P, 2, HEADS, DR], F32, name="tab")
+            magn = p1.tile([P, HEADS, HALF], F32, name="wagrp", bufs=4, align_bytes=64)
+
+            def tables():
+                nc.scalar.activation(out=magn[:], in_=tmp[:, 1], func=ACT.Abs)
+                nc.scalar.activation(out=tab[:, 1, :, 0:HALF], in_=tmp[:, 1], func=ACT.Sin, scale=2.0 * math.pi)
+                nc.scalar.activation(out=tab[:, 0, :, 0:HALF], in_=magn[:], func=ACT.Sin, scale=-2.0 * math.pi, bias=math.pi / 2.0)
+                for a in range(2):
+                    nc.gpsimd.tensor_scalar(out=tab[:, a, :, HALF:DR], in0=tab[:, a, :, 0:HALF], scalar1=1.0, scalar2=0.0, op0=ALU.mult, op1=ALU.add)
+
+            def words_out(dst_words, bank, n_g):
+                nc.scalar.copy(out=dst_words.rearrange("p (g r u) -> p g r u", g=n_g, u=2), in_=bank.rearrange("p g u r -> p g r u"))
+
+            x_codes, x_scales, x_grp = [], [], {}
+
+            def x_turn(m):
+                words = x_raw[m][:].bitcast(F32)
+                x_grp[m] = wb.tile([P, 4 * P * G1], BF16, name="grp", bufs=3, align_bytes=64)
+                gw = x_grp[m][:].bitcast(F32)
+                for b in range(2):
+                    bank = psum.tile([P, 2, 2, P], F32, name="tp", bufs=2)
+                    for gg in range(2):
+                        g = 2 * b + gg
+                        for u in range(2):
+                            nc.tensor.transpose(bank[:, gg, u, :], words[:, 256 * g + u:256 * (g + 1):2], ident_f[:])
+                    words_out(gw[:, 512 * b:512 * (b + 1)], bank[:], 2)
+
+            def x_quant(m):
+                codes = p1.tile([P, G1 * P], U32, name="xc%d" % m, align_bytes=64)
+                scales = p1.tile([P, G1 * P], U8, name="xs%d" % m, align_bytes=64)
+                nc.vector.quantize_mx(out=codes[:].bitcast(FP8X4), scales=scales[:], in_=x_grp[m][:])
+                x_codes.append(codes)
+                x_scales.append(scales)
+
+            wa_codes, wa_scales, wa_grp, acc = [], [], {}, {}
+            for g in range(G1):
+                wa_codes.append(p1.tile([P, QL], U32, name="wac%d" % g, align_bytes=64))
+                wa_scales.append(p1.tile([P, QL], U8, name="was%d" % g, align_bytes=64))
+
+            def wa_inter(g, n):
+                wa_grp[(g, n)] = p1.tile([P, 2048], BF16, name="wagrp", bufs=4, align_bytes=64)
+                interleave("s" if (g, n) in S_CHUNKS else "v", wa_grp[(g, n)][:], wa_raw[g][:, :, n * 512:(n + 1) * 512])
+
+            def wa_quant(g, n):
+                cols = slice(n * 512, (n + 1) * 512)
+                nc.vector.quantize_mx(out=wa_codes[g][:, cols].bitcast(FP8X4), scales=wa_scales[g][:, cols], in_=wa_grp[(g, n)][:])
+
+            def mm1(m, n, g):
+                if g == 0:
+                    acc[(m, n)] = psum.tile([P, 512], F32, name="acc", bufs=6)
+                nc.tensor.matmul_mx(
+                    out=acc[(m, n)][:],
+                    lhsT=x_codes[m][:, g * P:(g + 1) * P].bitcast(FP8X4),
+                    lhsT_scale=x_scales[m][:, g * P:(g + 1) * P],
+                    rhs=wa_codes[g][:, n * 512:(n + 1) * 512].bitcast(FP8X4),
+                    rhs_scale=wa_scales[g][:, n * 512:(n + 1) * 512],
+                    start=(g == 0), stop=(g == G1 - 1),
+                )
+
+            chunks = [(g, n) for g in range(G1) for n in range(3)]
+            advance(ADV0)
+            for i, (g, n) in enumerate(chunks):
+                if i == TAB_AT:
+                    tables()
+                if i in X_AT:
+                    x_turn(X_AT.index(i))
+                wa_inter(g, n)
+                if i > 0:
+                    wa_quant(*chunks[i - 1])
+                if i - 1 in X_AT:
+                    x_quant(X_AT.index(i - 1))
+                if (g, n) == (1, 2):
+                    for gn in chunks[:5]:
+                        for m in range(2):
+                            mm1(m, gn[1], gn[0])
+                elif i > 5:
+                    for m in range(2):
+                        mm1(m, chunks[i - 1][1], chunks[i - 1][0])
+                if n == 2 and g in (0, 1):
+                    load_wa()
+                    if g == 1:
+                        load_bytes()
+                        load_bytes()
+                        load_bytes()
+                        load_bytes()
+                advance(ADV1[i])
+            gain = const.tile([P, QL], BF16, name="gain")
+            for c0, w in ((0, 1024), (1024, 512)):
+                bank = psum.tile([P, 1024], BF16, name="tp", bufs=2)
+                for c in range(0, w, 512):
+                    nc.tensor.matmul(bank[:, c:c + 512], lhsT=ones_b[:], rhs=wrow[:, c0 + c:c0 + c + 512], start=True, stop=True)
+                nc.scalar.copy(out=gain[:, c0:c0 + w], in_=bank[:, 0:w])
+            wa_quant(*chunks[-1])
+            for m in range(2):
+                mm1(m, 2, 3)
+
+            cn_codes, cn_scales = [], []
+            ssq, rs, cn, cn_grp = {}, {}, {}, {}
+
+            def squares(m):
+                ssq[m] = const.tile([P, 4], F32, name="ssq%d" % m)
+                rs[m] = const.tile([P, 4], F32, name="rs%d" % m)
+                for n in range(3):
+                    junk = wb.tile([P, 512], BF16, name="junk", bufs=2)
+                    nc.scalar.activation(out=junk[:], in_=acc[(m, n)][:], func=ACT.Square, accum_out=ssq[m][:, n:n + 1])
+                s, r = ssq[m], rs[m]
+                nc.gpsimd.tensor_tensor(out=r[:, 0:1], in0=s[:, 0:1], in1=s[:, 1:2], op=ALU.add)
+                nc.gpsimd.tensor_tensor(out=r[:, 1:2], in0=r[:, 0:1], in1=s[:, 2:3], op=ALU.add)
+                nc.gpsimd.tensor_scalar(out=r[:, 2:3], in0=r[:, 1:2], scalar1=1.0 / QL, scalar2=EPS, op0=ALU.mult, op1=ALU.add)
+                nc.gpsimd.tensor_tensor(out=r[:, 3:4], in0=r[:, 2:3], in1=nhalf[:], op=ALU.pow)
+
+            def normed(m):
+                cn[m] = p1.tile([P, QL], BF16, name="wagrp", bufs=4, align_bytes=64)
+                for n in range(3):
+                    nc.vector.scalar_tensor_tensor(
+                        out=cn[m][:, n * 512:(n + 1) * 512], in0=acc[(m, n)][:], scalar=rs[m][:, 3:4],
+                        in1=gain[:, n * 512:(n + 1) * 512], op0=ALU.mult, op1=ALU.mult)
+
+            def cn_turn(m):
+                words = cn[m][:].bitcast(F32)
+                cn_grp[m] = p1.tile([P, 4 * P * G2], BF16, name="wagrp", bufs=4, align_bytes=64)
+                gw = cn_grp[m][:].bitcast(F32)
+                for g0, n_g in ((0, 2), (2, 1)):
+                    bank = psum.tile([P, 2, 2, P], F32, name="tp", bufs=2)
+                    for gg in range(n_g):
+                        for u in range(2):
+                            g = g0 + gg
+                            nc.tensor.transpose(bank[:, gg, u, :], words[:, 256 * g + u:256 * (g + 1):2], ident_f[:])
+                    words_out(gw[:, 256 * g0:256 * (g0 + n_g)], bank[:, 0:n_g], n_g)
+
+            def cn_quant(m):
+                codes = const.tile([P, G2 * P], U32, name="cc%d" % m, align_bytes=64)
+                scales = const.tile([P, G2 * P], U8, name="cs%d" % m, align_bytes=64)
+                for a, w in ((0, 256), (256, 128)):
+                    nc.vector.quantize_mx(out=codes[:, a:a + w].bitcast(FP8X4), scales=scales[:, a:a + w], in_=cn_grp[m][:, 4 * a:4 * (a + w)])
+                cn_codes.append(codes)
+                cn_scales.append(scales)
+
+            def mm1_tile(m):
+                for n in range(3):
+                    for g in range(G1):
+                        mm1(m, n, g)
+
+            A = ADVN
+            squares(0)
+            advance(A[0])
+            squares(1)
+            normed(0)
+            advance(A[1])
+            mm1_tile(2)
+            cn_turn(0)
+            normed(1)
+            advance(A[2])
+            squares(2)
+            mm1_tile(3)
+            cn_turn(1)
+            cn_quant(0)
+            advance(A[3])
+            squares(3)
+            normed(2)
+            cn_quant(1)
+            advance(A[4])
+            cn_turn(2)
+            normed(3)
+            advance(A[5])
+            cn_turn(3)
+            cn_quant(2)
+            advance(A[6])
+            cn_quant(3)
+
+        p2 = ctx.enter_context(tc.tile_pool(name="p2", bufs=1))
+        late.append(p2)
+        blocks = [(q, m) for q in range(NQ) for m in range(MT)]
+        banks = {}
+
+        def mm2(b):
+            q, m = blocks[b]
+            upto_unit(3 * q + 2)
+            for i in range(2):
+                bank = psum.tile([P, 2, HD], F32, name="acc", bufs=6)
+                banks[(b, i)] = bank
+                for g in range(G2):
+                    codes, scales = wb_codes[(q, g)]
+                    nc.tensor.matmul_mx(
+                        out=bank[:].rearrange("p h d -> p (h d)"),
+                        lhsT=cn_codes[m][:, g * P:(g + 1) * P].bitcast(FP8X4),
+                        lhsT_scale=cn_scales[m][:, g * P:(g + 1) * P],
+                        rhs=codes[:, i * 512:(i + 1) * 512].bitcast(FP8X4),
+                        rhs_scale=scales[:, i * 512:(i + 1) * 512],
+                        start=(g == 0), stop=(g == G2 - 1),
+                    )
+
+        o_tiles, prods = {}, {}
+
+        def evacuate(b):
+            q, m = blocks[b]
+            o = p2.tile([P, 4, HD], F32, name="o", bufs=4)
+            prod = p2.tile([P, 2, 4, DR], F32, name="prod", bufs=3)
+            o_tiles[b], prods[b] = o, prod
+            for i in range(2):
+                bank = banks[(b, i)]
+                h0 = 4 * q + 2 * i
+                nc.vector.tensor_tensor(
+                    out=prod[:, :, 2 * i:2 * i + 2, :],
+                    in0=bank[:, :, DR:HD].unsqueeze(1).to_broadcast([P, 2, 2, DR]),
+                    in1=tab[:, :, h0:h0 + 2, :], op=ALU.mult)
+                nc.scalar.copy(out=o[:, 2 * i:2 * i + 2, 0:DR], in_=bank[:, :, 0:DR])
+
+        def rotate(b):
+            q, m = blocks[b]
+            o, prod = o_tiles[b], prods[b]
+            eng = nc.gpsimd if b in GP_ADDS else nc.vector
+            eng.tensor_tensor(out=o[:, :, DR:DR + HALF], in0=prod[:, 0, :, 0:HALF], in1=prod[:, 1, :, HALF:DR], op=ALU.subtract)
+            eng.tensor_tensor(out=o[:, :, DR + HALF:HD], in0=prod[:, 0, :, HALF:DR], in1=prod[:, 1, :, 0:HALF], op=ALU.add)
+            nc.sync.dma_start(out=out_rows[m * P:(m + 1) * P, q * QW:(q + 1) * QW], in_=o[:].rearrange("p h d -> p (h d)"))
+
+        AB = ADVB
+        mm2(0)
+        for b in range(len(blocks)):
+            if b + 1 < len(blocks):
+                mm2(b + 1)
+            evacuate(b)
+            advance(AB[b])
+            if b > 0:
+                rotate(b - 1)
+        rotate(len(blocks) - 1)

@@ -29,18 +29,20 @@ NQ = 4
 QW = OUT // NQ
 
 UNITS = [(q, g) for q in range(NQ) for g in range(G2)]
-PE_UNITS = {(1, 1), (1, 2), (2, 1), (2, 2), (3, 1), (3, 2)}
-V_WIDEN = [4, 2, 0, 1, 3, 3, 0, 2, 2, 0, 1, 2]
-S_CHUNKS = {(0, 1), (1, 2), (2, 0), (3, 1), (3, 2)}
+PE_UNITS = {(1, 0), (1, 2), (2, 1), (2, 2), (3, 1), (3, 2)}
+V_WIDEN = [3, 3, 0, 1, 2, 3, 3, 1, 0, 4, 0, 3]
+S_CHUNKS = {(0, 1), (1, 2), (2, 1), (3, 1), (3, 2)}
 
 X_AT = [0, 1, 2, 3]
 ADV0 = 4
 ADV1 = [0, 0, 0, 0, 0, 0, 0, 0, 0, 1, 0, 0]
-ADVN = [1, 6, 2, 2, 4, 4, 2]
-ADVB = [2, 3, 1, 3, 2, 3, 0, 1, 2, 2, 2, 0, 2, 1, 4, 4]
+ADVN = [2, 5, 4, 1, 7, 5, 1]
+ADVB = [1, 2, 0, 3, 5, 2, 1, 1, 2, 6, 3, 1, 5, 3, 7, 1]
 GP_ADDS = (12, 13, 14, 15)
+LEAD = 5
+NB0 = 2
 EARLY_UNITS = 5
-QUANT_AT = 2
+QUANT_AT = 1
 TAB_AT = 9
 
 
@@ -96,8 +98,8 @@ def tile_mla_pa_kernel(tc, x, wq_a, q_norm_w, wq_b_bytes, wq_b_scale, out):
                 bank = psum.tile([P, 1024], BF16, name="tp", bufs=2)
                 for i in range(2):
                     c0 = 256 * j + 128 * i
-                    nc.tensor.matmul(bank[:, 512 * i:512 * (i + 1)], lhsT=ident_b[:],
-                                     rhs=planes[:, :, c0:c0 + 128].rearrange("p t c -> p c t"), start=True, stop=True)
+                    nc.tensor.matmul(bank[:, 512 * i:512 * (i + 1)].rearrange("p (c t) -> p t c", t=4), lhsT=ident_b[:],
+                                     rhs=planes[:, :, c0:c0 + 128], start=True, stop=True)
                 nc.scalar.copy(out=grp[:, 1024 * j:1024 * (j + 1)], in_=bank[:])
             elif j % 2 == 1:
                 interleave("v", grp[:, 1024 * (j - 1):1024 * (j + 1)], planes[:, :, 256 * (j - 1):256 * (j + 1)])
@@ -109,23 +111,23 @@ def tile_mla_pa_kernel(tc, x, wq_a, q_norm_w, wq_b_bytes, wq_b_scale, out):
             nc.vector.quantize_mx(out=codes[:].bitcast(FP8X4), scales=scales[:], in_=group_tiles[k][:])
             wb_codes[UNITS[k]] = (codes, scales)
 
-        STEPS = 4 + 4 * len(UNITS) + 1
+        STEPS = LEAD + 4 * len(UNITS) + 1
         done = []
 
         def background(s):
-            if s < 4:
-                widen(0, s)
+            if s < 4 * len(UNITS):
+                widen(s // 4, s % 4)
+            if s < LEAD:
                 return
-            k, j = divmod(s - 4, 4)
+            k, j = divmod(s - LEAD, 4)
             if k == len(UNITS):
                 quantise_unit(k - 1)
                 return
-            if k + 1 < len(UNITS):
-                widen(k + 1, j)
             part(k, j)
+            if j == 3:
+                load_bytes()
             if j == QUANT_AT and k > 0:
                 quantise_unit(k - 1)
-                load_bytes()
 
         def advance(n):
             for _ in range(min(n, STEPS - len(done))):
@@ -275,10 +277,8 @@ def tile_mla_pa_kernel(tc, x, wq_a, q_norm_w, wq_b_bytes, wq_b_scale, out):
                 if n == 2 and g in (0, 1):
                     load_wa()
                     if g == 1:
-                        load_bytes()
-                        load_bytes()
-                        load_bytes()
-                        load_bytes()
+                        for _ in range(5 - NB0):
+                            load_bytes()
                 advance(ADV1[i])
             gain = const.tile([P, QL], BF16, name="gain")
             for c0, w in ((0, 1024), (1024, 512)):

import math
from contextlib import ExitStack

import concourse.mybir as mybir
from concourse.masks import make_identity

F32 = mybir.dt.float32
BF16 = mybir.dt.bfloat16
I32 = mybir.dt.int32
U32 = mybir.dt.uint32
U8 = mybir.dt.uint8
FP8 = mybir.dt.float8_e4m3fn
FP8X4 = mybir.dt.float8_e4m3fn_x4
ALU = mybir.AluOpType
ACT = mybir.ActivationFunctionType

P = 128
TOK, DIM, QL, OUT = 512, 2048, 1536, 4096
HEADS, HD, DR = 16, 256, 128
HALF = DR // 2
POS0 = 37
EPS = 1e-6
FLOPS = 2 * TOK * DIM * QL + 2 * TOK * QL * OUT

MT = TOK // P
G1 = DIM // 512
G2 = QL // 512
NQ = 4
QW = OUT // NQ

UNITS = [(q, g) for q in range(NQ) for g in range(G2)]
PE_UNITS = {(1, 0), (1, 2), (2, 1), (2, 2), (3, 1), (3, 2)}
V_WIDEN = [3, 3, 0, 1, 2, 3, 3, 1, 0, 4, 0, 3]
S_CHUNKS = {(0, 1), (1, 2), (2, 1), (3, 1), (3, 2)}

X_AT = [0, 1, 2, 3]
ADV0 = 4
ADV1 = [0, 0, 0, 0, 0, 0, 0, 0, 0, 1, 0, 0]
ADVN = [2, 5, 4, 1, 7, 5, 1]
ADVB = [1, 2, 0, 3, 5, 2, 1, 1, 2, 6, 3, 1, 5, 3, 7, 1]
GP_ADDS = (12, 13, 14, 15)
LEAD = 5
NB0 = 2
EARLY_UNITS = 5
QUANT_AT = 1
TAB_AT = 9


def tile_mla_pa_kernel(tc, x, wq_a, q_norm_w, wq_b_bytes, wq_b_scale, out):
    nc = tc.nc
    x_rows = x.rearrange("b s d -> (b s) d")
    out_rows = out.rearrange("b s h c -> (b s) (h c)")

    with ExitStack() as ctx:
        const = ctx.enter_context(tc.tile_pool(name="const", bufs=1))
        wb = ctx.enter_context(tc.tile_pool(name="wb", bufs=1))
        psum = ctx.enter_context(tc.psum_pool(name="psum", bufs=1))
        ctx.enter_context(tc.manual_schedule())

        sc = const.tile([P, G2, 4], F32, name="sc")
        byte_tiles, plane_tiles, group_tiles, wb_codes = {}, {}, {}, {}
        loaded, late = [], []

        def load_bytes():
            if len(loaded) == len(UNITS):
                return
            q, g = UNITS[len(loaded)]
            b = wb.tile([P, 4, QW], U8, name="wbytes", bufs=5)
            rows = wq_b_bytes[g * 512:(g + 1) * 512, q * QW:(q + 1) * QW]
            nc.sync.dma_start(out=b[:], in_=rows.rearrange("(p t) n -> p t n", t=4))
            byte_tiles[(q, g)] = b
            loaded.append((q, g))

        def widen(k, t):
            q, g = UNITS[k]
            if t == 0:
                plane_tiles[k] = wb.tile([P, 4, QW], BF16, name="planes", bufs=3, align_bytes=64)
            planes = plane_tiles[k]
            src = byte_tiles[(q, g)][:, t, :].bitcast(FP8)
            if t < V_WIDEN[k]:
                nc.vector.tensor_scalar(out=planes[:, t, :], in0=src, scalar1=sc[:, g, t:t + 1], scalar2=None, op0=ALU.mult)
            else:
                nc.scalar.activation(out=planes[:, t, :], in_=src, func=ACT.Copy, scale=sc[:, g, t:t + 1])

        def interleave(eng, dst, src):
            d = dst.rearrange("p (c i t) -> p c t i", i=4, t=4)
            s = src.rearrange("p t (c i) -> p c t i", i=4)
            if eng == "v":
                nc.vector.tensor_copy(out=d, in_=s)
            else:
                nc.scalar.copy(out=d, in_=s)

        def part(k, j):
            if j == 0:
                group_tiles[k] = wb.tile([P, 4 * QW], BF16, name="grp", bufs=3, align_bytes=64)
            planes, grp = plane_tiles[k], group_tiles[k]
            if UNITS[k] in PE_UNITS:
                bank = psum.tile([P, 1024], BF16, name="tp", bufs=2)
                for i in range(2):
                    c0 = 256 * j + 128 * i
                    nc.tensor.matmul(bank[:, 512 * i:512 * (i + 1)].rearrange("p (c t) -> p t c", t=4), lhsT=ident_b[:],
                                     rhs=planes[:, :, c0:c0 + 128], start=True, stop=True)
                nc.scalar.copy(out=grp[:, 1024 * j:1024 * (j + 1)], in_=bank[:])
            elif j % 2 == 1:
                interleave("v", grp[:, 1024 * (j - 1):1024 * (j + 1)], planes[:, :, 256 * (j - 1):256 * (j + 1)])

        def quantise_unit(k):
            pool = wb if k < EARLY_UNITS else late[0]
            codes = pool.tile([P, QW], U32, name="wbc%d" % k, align_bytes=64)
            scales = pool.tile([P, QW], U8, name="wbs%d" % k, align_bytes=64)
            nc.vector.quantize_mx(out=codes[:].bitcast(FP8X4), scales=scales[:], in_=group_tiles[k][:])
            wb_codes[UNITS[k]] = (codes, scales)

        STEPS = LEAD + 4 * len(UNITS) + 1
        done = []

        def background(s):
            if s < 4 * len(UNITS):
                widen(s // 4, s % 4)
            if s < LEAD:
                return
            k, j = divmod(s - LEAD, 4)
            if k == len(UNITS):
                quantise_unit(k - 1)
                return
            part(k, j)
            if j == 3:
                load_bytes()
            if j == QUANT_AT and k > 0:
                quantise_unit(k - 1)

        def advance(n):
            for _ in range(min(n, STEPS - len(done))):
                background(len(done))
                done.append(0)

        def upto_unit(k):
            while UNITS[k] not in wb_codes:
                advance(1)

        with tc.tile_pool(name="p1", bufs=1) as p1:
            nc.sync.dma_start(out=sc[:], in_=wq_b_scale.rearrange("(g p t) o -> p g (t o)", p=P, t=4))
            x_raw, wa_raw = [], []

            def load_x():
                m = len(x_raw)
                r = p1.tile([P, DIM], BF16, name="xraw", bufs=4)
                nc.sync.dma_start(out=r[:], in_=x_rows[m * P:(m + 1) * P, :])
                x_raw.append(r)

            def load_wa():
                g = len(wa_raw)
                r = p1.tile([P, 4, QL], BF16, name="waraw", bufs=2)
                nc.sync.dma_start(out=r[:], in_=wq_a[g * 512:(g + 1) * 512, :].rearrange("(p t) n -> p t n", t=4))
                wa_raw.append(r)

            load_bytes()
            load_wa()
            load_x()
            load_x()
            load_x()
            load_x()
            load_wa()
            wrow = p1.tile([P, QL], BF16, name="wrow", align_bytes=64)
            nc.gpsimd.memset(wrow[:], 0.0)
            nc.sync.dma_start(out=wrow[0:1, :], in_=q_norm_w.rearrange("(o n) -> o n", o=1))

            ident_f = const.tile([P, P], F32, name="ident_f")
            make_identity(nc, ident_f[:])
            ones_b = const.tile([P, P], BF16, name="ones_b")
            nc.gpsimd.memset(ones_b[:], 1.0)
            nhalf = const.tile([P, 1], F32, name="nhalf")
            nc.gpsimd.memset(nhalf[:], -0.5)

            freq = const.tile([P, HALF], F32, name="freq")
            posi = const.tile([P, HEADS], I32, name="posi")
            posm = const.tile([P, HEADS], I32, name="posm")
            post = const.tile([P, HEADS], F32, name="post")
            nc.gpsimd.iota(posi[:], pattern=[[1, HEADS]], base=0, channel_multiplier=16)
            nc.vector.memset(freq[:, 0:1], 1.0)
            n = 1
            while n < HALF:
                nc.vector.tensor_scalar(out=freq[:, n:2 * n], in0=freq[:, 0:n], scalar1=10000.0 ** (-n / HALF), scalar2=None, op0=ALU.mult)
                n *= 2
            nc.vector.tensor_scalar(out=posm[:], in0=posi[:], scalar1=255, scalar2=None, op0=ALU.bitwise_and)
            nc.vector.tensor_scalar(out=post[:], in0=posm[:], scalar1=float(POS0), scalar2=1.0 / (2.0 * math.pi), op0=ALU.add, op1=ALU.mult)
            tmp = wb.tile([P, 2, HEADS, HALF], F32, name="planes", bufs=3, align_bytes=64)
            whole = p1.tile([P, HEADS, HALF], I32, name="wagrp", bufs=4, align_bytes=64)
            nc.gpsimd.tensor_tensor(
                out=tmp[:, 0],
                in0=post[:].unsqueeze(2).to_broadcast([P, HEADS, HALF]),
                in1=freq[:].unsqueeze(1).to_broadcast([P, HEADS, HALF]),
                op=ALU.mult,
            )
            nc.vector.tensor_copy(out=whole[:], in_=tmp[:, 0])
            nc.vector.tensor_tensor(out=tmp[:, 1], in0=tmp[:, 0], in1=whole[:], op=ALU.subtract)
            ident_b = const.tile([P, P], BF16, name="ident_b")
            nc.vector.tensor_copy(out=ident_b[:], in_=ident_f[:])
            tab = const.tile([P, 2, HEADS, DR], F32, name="tab")
            magn = p1.tile([P, HEADS, HALF], F32, name="wagrp", bufs=4, align_bytes=64)

            def tables():
                nc.scalar.activation(out=magn[:], in_=tmp[:, 1], func=ACT.Abs)
                nc.scalar.activation(out=tab[:, 1, :, 0:HALF], in_=tmp[:, 1], func=ACT.Sin, scale=2.0 * math.pi)
                nc.scalar.activation(out=tab[:, 0, :, 0:HALF], in_=magn[:], func=ACT.Sin, scale=-2.0 * math.pi, bias=math.pi / 2.0)
                for a in range(2):
                    nc.gpsimd.tensor_scalar(out=tab[:, a, :, HALF:DR], in0=tab[:, a, :, 0:HALF], scalar1=1.0, scalar2=0.0, op0=ALU.mult, op1=ALU.add)

            def words_out(dst_words, bank, n_g):
                nc.scalar.copy(out=dst_words.rearrange("p (g r u) -> p g r u", g=n_g, u=2), in_=bank.rearrange("p g u r -> p g r u"))

            x_codes, x_scales, x_grp = [], [], {}

            def x_turn(m):
                words = x_raw[m][:].bitcast(F32)
                x_grp[m] = wb.tile([P, 4 * P * G1], BF16, name="grp", bufs=3, align_bytes=64)
                gw = x_grp[m][:].bitcast(F32)
                for b in range(2):
                    bank = psum.tile([P, 2, 2, P], F32, name="tp", bufs=2)
                    for gg in range(2):
                        g = 2 * b + gg
                        for u in range(2):
                            nc.tensor.transpose(bank[:, gg, u, :], words[:, 256 * g + u:256 * (g + 1):2], ident_f[:])
                    words_out(gw[:, 512 * b:512 * (b + 1)], bank[:], 2)

            def x_quant(m):
                codes = p1.tile([P, G1 * P], U32, name="xc%d" % m, align_bytes=64)
                scales = p1.tile([P, G1 * P], U8, name="xs%d" % m, align_bytes=64)
                nc.vector.quantize_mx(out=codes[:].bitcast(FP8X4), scales=scales[:], in_=x_grp[m][:])
                x_codes.append(codes)
                x_scales.append(scales)

            wa_codes, wa_scales, wa_grp, acc = [], [], {}, {}
            for g in range(G1):
                wa_codes.append(p1.tile([P, QL], U32, name="wac%d" % g, align_bytes=64))
                wa_scales.append(p1.tile([P, QL], U8, name="was%d" % g, align_bytes=64))

            def wa_inter(g, n):
                wa_grp[(g, n)] = p1.tile([P, 2048], BF16, name="wagrp", bufs=4, align_bytes=64)
                interleave("s" if (g, n) in S_CHUNKS else "v", wa_grp[(g, n)][:], wa_raw[g][:, :, n * 512:(n + 1) * 512])

            def wa_quant(g, n):
                cols = slice(n * 512, (n + 1) * 512)
                nc.vector.quantize_mx(out=wa_codes[g][:, cols].bitcast(FP8X4), scales=wa_scales[g][:, cols], in_=wa_grp[(g, n)][:])

            def mm1(m, n, g):
                if g == 0:
                    acc[(m, n)] = psum.tile([P, 512], F32, name="acc", bufs=6)
                nc.tensor.matmul_mx(
                    out=acc[(m, n)][:],
                    lhsT=x_codes[m][:, g * P:(g + 1) * P].bitcast(FP8X4),
                    lhsT_scale=x_scales[m][:, g * P:(g + 1) * P],
                    rhs=wa_codes[g][:, n * 512:(n + 1) * 512].bitcast(FP8X4),
                    rhs_scale=wa_scales[g][:, n * 512:(n + 1) * 512],
                    start=(g == 0), stop=(g == G1 - 1),
                )

            chunks = [(g, n) for g in range(G1) for n in range(3)]
            advance(ADV0)
            for i, (g, n) in enumerate(chunks):
                if i == TAB_AT:
                    tables()
                if i in X_AT:
                    x_turn(X_AT.index(i))
                wa_inter(g, n)
                if i > 0:
                    wa_quant(*chunks[i - 1])
                if i - 1 in X_AT:
                    x_quant(X_AT.index(i - 1))
                if (g, n) == (1, 2):
                    for gn in chunks[:5]:
                        for m in range(2):
                            mm1(m, gn[1], gn[0])
                elif i > 5:
                    for m in range(2):
                        mm1(m, chunks[i - 1][1], chunks[i - 1][0])
                if n == 2 and g in (0, 1):
                    load_wa()
                    if g == 1:
                        for _ in range(5 - NB0):
                            load_bytes()
                advance(ADV1[i])
            gain = const.tile([P, QL], BF16, name="gain")
            for c0, w in ((0, 1024), (1024, 512)):
                bank = psum.tile([P, 1024], BF16, name="tp", bufs=2)
                for c in range(0, w, 512):
                    nc.tensor.matmul(bank[:, c:c + 512], lhsT=ones_b[:], rhs=wrow[:, c0 + c:c0 + c + 512], start=True, stop=True)
                nc.scalar.copy(out=gain[:, c0:c0 + w], in_=bank[:, 0:w])
            wa_quant(*chunks[-1])
            for m in range(2):
                mm1(m, 2, 3)

            cn_codes, cn_scales = [], []
            ssq, rs, cn, cn_grp = {}, {}, {}, {}

            def squares(m):
                ssq[m] = const.tile([P, 4], F32, name="ssq%d" % m)
                rs[m] = const.tile([P, 4], F32, name="rs%d" % m)
                for n in range(3):
                    junk = wb.tile([P, 512], BF16, name="junk", bufs=2)
                    nc.scalar.activation(out=junk[:], in_=acc[(m, n)][:], func=ACT.Square, accum_out=ssq[m][:, n:n + 1])
                s, r = ssq[m], rs[m]
                nc.gpsimd.tensor_tensor(out=r[:, 0:1], in0=s[:, 0:1], in1=s[:, 1:2], op=ALU.add)
                nc.gpsimd.tensor_tensor(out=r[:, 1:2], in0=r[:, 0:1], in1=s[:, 2:3], op=ALU.add)
                nc.gpsimd.tensor_scalar(out=r[:, 2:3], in0=r[:, 1:2], scalar1=1.0 / QL, scalar2=EPS, op0=ALU.mult, op1=ALU.add)
                nc.gpsimd.tensor_tensor(out=r[:, 3:4], in0=r[:, 2:3], in1=nhalf[:], op=ALU.pow)

            def normed(m):
                cn[m] = p1.tile([P, QL], BF16, name="wagrp", bufs=4, align_bytes=64)
                for n in range(3):
                    nc.vector.scalar_tensor_tensor(
                        out=cn[m][:, n * 512:(n + 1) * 512], in0=acc[(m, n)][:], scalar=rs[m][:, 3:4],
                        in1=gain[:, n * 512:(n + 1) * 512], op0=ALU.mult, op1=ALU.mult)

            def cn_turn(m):
                words = cn[m][:].bitcast(F32)
                cn_grp[m] = p1.tile([P, 4 * P * G2], BF16, name="wagrp", bufs=4, align_bytes=64)
                gw = cn_grp[m][:].bitcast(F32)
                for g0, n_g in ((0, 2), (2, 1)):
                    bank = psum.tile([P, 2, 2, P], F32, name="tp", bufs=2)
                    for gg in range(n_g):
                        for u in range(2):
                            g = g0 + gg
                            nc.tensor.transpose(bank[:, gg, u, :], words[:, 256 * g + u:256 * (g + 1):2], ident_f[:])
                    words_out(gw[:, 256 * g0:256 * (g0 + n_g)], bank[:, 0:n_g], n_g)

            def cn_quant(m):
                codes = const.tile([P, G2 * P], U32, name="cc%d" % m, align_bytes=64)
                scales = const.tile([P, G2 * P], U8, name="cs%d" % m, align_bytes=64)
                for a, w in ((0, 256), (256, 128)):
                    nc.vector.quantize_mx(out=codes[:, a:a + w].bitcast(FP8X4), scales=scales[:, a:a + w], in_=cn_grp[m][:, 4 * a:4 * (a + w)])
                cn_codes.append(codes)
                cn_scales.append(scales)

            def mm1_tile(m):
                for n in range(3):
                    for g in range(G1):
                        mm1(m, n, g)

            A = ADVN
            squares(0)
            advance(A[0])
            squares(1)
            normed(0)
            advance(A[1])
            mm1_tile(2)
            cn_turn(0)
            normed(1)
            advance(A[2])
            squares(2)
            mm1_tile(3)
            cn_turn(1)
            cn_quant(0)
            advance(A[3])
            squares(3)
            normed(2)
            cn_quant(1)
            advance(A[4])
            cn_turn(2)
            normed(3)
            advance(A[5])
            cn_turn(3)
            cn_quant(2)
            advance(A[6])
            cn_quant(3)

        p2 = ctx.enter_context(tc.tile_pool(name="p2", bufs=1))
        late.append(p2)
        blocks = [(q, m) for q in range(NQ) for m in range(MT)]
        banks = {}

        def mm2(b):
            q, m = blocks[b]
            upto_unit(3 * q + 2)
            for i in range(2):
                bank = psum.tile([P, 2, HD], F32, name="acc", bufs=6)
                banks[(b, i)] = bank
                for g in range(G2):
                    codes, scales = wb_codes[(q, g)]
                    nc.tensor.matmul_mx(
                        out=bank[:].rearrange("p h d -> p (h d)"),
                        lhsT=cn_codes[m][:, g * P:(g + 1) * P].bitcast(FP8X4),
                        lhsT_scale=cn_scales[m][:, g * P:(g + 1) * P],
                        rhs=codes[:, i * 512:(i + 1) * 512].bitcast(FP8X4),
                        rhs_scale=scales[:, i * 512:(i + 1) * 512],
                        start=(g == 0), stop=(g == G2 - 1),
                    )

        o_tiles, prods = {}, {}

        def evacuate(b):
            q, m = blocks[b]
            o = p2.tile([P, 4, HD], F32, name="o", bufs=4)
            prod = p2.tile([P, 2, 4, DR], F32, name="prod", bufs=3)
            o_tiles[b], prods[b] = o, prod
            for i in range(2):
                bank = banks[(b, i)]
                h0 = 4 * q + 2 * i
                nc.vector.tensor_tensor(
                    out=prod[:, :, 2 * i:2 * i + 2, :],
                    in0=bank[:, :, DR:HD].unsqueeze(1).to_broadcast([P, 2, 2, DR]),
                    in1=tab[:, :, h0:h0 + 2, :], op=ALU.mult)
                nc.scalar.copy(out=o[:, 2 * i:2 * i + 2, 0:DR], in_=bank[:, :, 0:DR])

        def rotate(b):
            q, m = blocks[b]
            o, prod = o_tiles[b], prods[b]
            eng = nc.gpsimd if b in GP_ADDS else nc.vector
            eng.tensor_tensor(out=o[:, :, DR:DR + HALF], in0=prod[:, 0, :, 0:HALF], in1=prod[:, 1, :, HALF:DR], op=ALU.subtract)
            eng.tensor_tensor(out=o[:, :, DR + HALF:HD], in0=prod[:, 0, :, HALF:DR], in1=prod[:, 1, :, 0:HALF], op=ALU.add)
            nc.sync.dma_start(out=out_rows[m * P:(m + 1) * P, q * QW:(q + 1) * QW], in_=o[:].rearrange("p h d -> p (h d)"))

        AB = ADVB
        mm2(0)
        for b in range(len(blocks)):
            if b + 1 < len(blocks):
                mm2(b + 1)
            evacuate(b)
            advance(AB[b])
            if b > 0:
                rotate(b - 1)
        rotate(len(blocks) - 1)
